import numpy as np
import ml_dtypes

BF16 = ml_dtypes.bfloat16


def bf(x):
    return np.asarray(x, np.float32).astype(BF16)


def f32(x):
    return np.asarray(x, np.float32)


def f64(x):
    return np.asarray(x).astype(np.float64)


def striped(idx):
    return np.tile(idx.reshape(-1, 16).T, (8, 1))


C, S, N = 256, 2048, 512
EPS = 1e-6


def setup_inputs():
    return {"emb": f32(np.random.standard_normal((C, S))), "q": f32(np.random.standard_normal((C, N))), "k": f32(np.random.standard_normal((C, N))), "v": f32(np.random.standard_normal((C, N))), "offs": striped(np.random.permutation(S)[:N])}


def reference(emb, q, k, v, offs):
    idx = offs[:16].T.reshape(-1)
    e = f64(emb)[:, idx]
    qe = e + f64(q)
    ke = e + f64(k)
    ve = e + f64(v)
    s = qe.T @ ke / np.sqrt(C)
    mu = s.mean(axis=1, keepdims=True)
    sd = np.sqrt(((s - mu) ** 2).sum(axis=1, keepdims=True) / (N - 1))
    z = (s - mu) / (sd + EPS)
    p = np.exp(z - z.max(axis=1, keepdims=True))
    p = p / p.sum(axis=1, keepdims=True)
    return ve @ p.T

@@ -1,0 +1,143 @@
+import math
+
+import concourse.mybir as mybir
+from concourse.masks import make_identity
+
+P = 128
+C, S, N = 256, 2048, 512
+CB = C // P
+NB = N // P
+HALVES = 2
+HB = NB // HALVES
+EPS = 1e-6
+
+FLOPS = 2 * 2 * N * N * C
+BYTES = 4 * (C * N + 3 * C * N + C * N) + 2 * P * (N // 16)
+
+F32, BF16, U16 = mybir.dt.float32, mybir.dt.bfloat16, mybir.dt.uint16
+ADD, MULT, POW = mybir.AluOpType.add, mybir.AluOpType.mult, mybir.AluOpType.pow
+EXP = mybir.ActivationFunctionType.Exp
+
+
+def tile_neuromodulatedattentionwithelectrodes_kernel(tc, emb, q, k, v, offs, out):
+    nc = tc.nc
+    with (
+        tc.tile_pool(name="held", bufs=1) as held,
+        tc.psum_pool(name="scores", bufs=NB) as scores,
+        tc.psum_pool(name="flipped", bufs=NB) as flipped,
+    ):
+        offsets = held.tile([P, N // 16], U16, name="offsets")
+        nc.sync.dma_start(offsets[:], offs)
+        table = [held.tile([P, S], F32, name=f"table{cb}") for cb in range(CB)]
+        plain = {
+            (name, cb): held.tile([P, N], F32, name=f"{name}{cb}") for name in "kqv" for cb in range(CB)
+        }
+        for cb in range(CB):
+            channels = slice(cb * P, (cb + 1) * P)
+            nc.sync.dma_start(table[cb][:], emb[channels, :])
+            for name, source in (("k", k), ("q", q)):
+                nc.sync.dma_start(plain[name, cb][:], source[channels, :])
+        for cb in range(CB):
+            nc.sync.dma_start(plain["v", cb][:], v[cb * P : (cb + 1) * P, :])
+
+        identity32 = held.tile([P, P], F32, name="identity32")
+        make_identity(nc, identity32[:])
+        identity16 = held.tile([P, P], BF16, name="identity16")
+        make_identity(nc, identity16[:])
+        half = held.tile([P, 1], F32, name="half")
+        nc.gpsimd.memset(half[:], 0.5)
+        warm = held.tile([P, 1], F32, name="warm")
+        nc.scalar.activation(warm[:], half[:], EXP)
+
+        summed = {}
+        rounded = {}
+        veT = []
+        s_ps = [scores.tile([P, N], F32, name=f"s_ps{jb}", tag="s_ps") for jb in range(NB)]
+        for cb in range(CB):
+            for name in "kq":
+                summed[name, cb] = held.tile([P, N], F32, name=f"{name}e32_{cb}")
+                nc.vector.tensor_tensor(
+                    summed[name, cb][:], table[cb][:].indirect(offsets[:]), plain[name, cb][:], ADD
+                )
+            for name in "kq":
+                rounded[name, cb] = held.tile([P, N], BF16, name=f"{name}e16_{cb}")
+                nc.scalar.copy(rounded[name, cb][:], summed[name, cb][:])
+            for jb in range(NB):
+                nc.tensor.matmul(
+                    s_ps[jb][:],
+                    rounded["q", cb][:, jb * P : (jb + 1) * P],
+                    rounded["k", cb][:],
+                    start=(cb == 0),
+                    stop=(cb == CB - 1),
+                )
+        for cb in range(CB):
+            summed["v", cb] = held.tile([P, N], F32, name=f"ve32_{cb}")
+            nc.vector.tensor_tensor(summed["v", cb][:], table[cb][:].indirect(offsets[:]), plain["v", cb][:], ADD)
+            veT_ps = flipped.tile([P, NB, P], F32, name="veT_ps", tag="flip")
+            for ib in range(NB):
+                nc.tensor.transpose(veT_ps[:, ib, :], summed["v", cb][:, ib * P : (ib + 1) * P], identity32[:])
+            veT.append(held.tile([P, NB, P], BF16, name=f"veT{cb}"))
+            nc.scalar.copy(veT[cb][:], veT_ps[:])
+
+        idle_ps = flipped.tile([P, N], F32, name="idle_ps", tag="flip")
+        for repeat in range(12):
+            nc.tensor.matmul(idle_ps[:], identity16[:], rounded["k", CB - 1][:], start=True, stop=True)
+
+        mean_var, root, gain, shift, e, e_sum, p, pT_ps = {}, {}, {}, {}, {}, {}, {}, {}
+        out_blocks = out.rearrange("(cb p) j -> p cb j", p=P)
+
+        def measure(jb):
+            stats = held.tile([P, 6], F32, name=f"stats{jb}")
+            nc.vector.bn_stats(stats[:], s_ps[jb][:])
+            mean_var[jb] = held.tile([P, 2], F32, name=f"mean_var{jb}")
+            nc.vector.bn_aggr(mean_var[jb][:], stats[:])
+            root[jb] = held.tile([P, 1], F32, name=f"root{jb}")
+            nc.gpsimd.tensor_tensor(root[jb][:], mean_var[jb][:, 1:2], half[:], POW)
+
+        def exponentiate(jb):
+            gain[jb] = held.tile([P, 1], F32, name=f"gain{jb}")
+            nc.vector.tensor_scalar(
+                gain[jb][:], root[jb][:], math.sqrt(N / (N - 1)), math.sqrt(C) * EPS, MULT, ADD
+            )
+            nc.vector.reciprocal(gain[jb][:], gain[jb][:])
+            shift[jb] = held.tile([P, 1], F32, name=f"shift{jb}")
+            nc.vector.tensor_scalar(shift[jb][:], mean_var[jb][:, 0:1], gain[jb][:], -1.0, MULT, MULT)
+            e[jb] = held.tile([P, N], F32, name=f"e{jb}")
+            e_sum[jb] = held.tile([P, 1], F32, name=f"e_sum{jb}")
+            nc.scalar.activation(
+                e[jb][:], s_ps[jb][:], EXP, bias=shift[jb][:], scale=gain[jb][:], accum_out=e_sum[jb][:]
+            )
+
+        def normalise_and_flip(jb):
+            nc.vector.reciprocal(e_sum[jb][:], e_sum[jb][:])
+            p[jb] = held.tile([P, N], BF16, name=f"p{jb}")
+            nc.vector.tensor_scalar(p[jb][:], e[jb][:], e_sum[jb][:], None, MULT)
+            for h in range(HALVES):
+                pT_ps[jb, h] = flipped.tile([P, HB, P], BF16, name=f"pT_ps{jb}_{h}", tag="flip")
+                for hb in range(HB):
+                    ib = h * HB + hb
+                    nc.tensor.transpose(pT_ps[jb, h][:, hb, :], p[jb][:, ib * P : (ib + 1) * P], identity16[:])
+
+        def weigh_and_store(jb):
+            pT = {}
+            for h in range(HALVES):
+                pT[h] = held.tile([P, HB, P], BF16, name=f"pT{jb}_{h}")
+            nc.vector.tensor_copy(pT[0][:], pT_ps[jb, 0][:])
+            nc.scalar.copy(pT[1][:], pT_ps[jb, 1][:])
+            o_ps = scores.tile([P, CB, P], F32, name=f"o_ps{jb}", tag="s_ps")
+            for cb in range(CB):
+                for ib in range(NB):
+                    nc.tensor.matmul(
+                        o_ps[:, cb, :],
+                        veT[cb][:, ib, :],
+                        pT[ib // HB][:, ib % HB, :],
+                        start=(ib == 0),
+                        stop=(ib == NB - 1),
+                    )
+            o = held.tile([P, CB, P], F32, name=f"o{jb}")
+            nc.scalar.copy(o[:], o_ps[:])
+            nc.sync.dma_start(out_blocks[:, :, jb * P : (jb + 1) * P], o[:])
+
+        for stage in (measure, exponentiate, normalise_and_flip, weigh_and_store):
+            for jb in range(NB):
+                stage(jb)

@@ -138,6 +138,12 @@ def tile_neuromodulatedattentionwithelectrodes_kernel(tc, emb, q, k, v, offs, ou
             nc.scalar.copy(o[:], o_ps[:])
             nc.sync.dma_start(out_blocks[:, :, jb * P : (jb + 1) * P], o[:])
 
-        for stage in (measure, exponentiate, normalise_and_flip, weigh_and_store):
-            for jb in range(NB):
-                stage(jb)
+        for jb in range(NB):
+            measure(jb)
+        for jb in range(NB):
+            exponentiate(jb)
+        for jb in range(NB):
+            normalise_and_flip(jb)
+            if jb >= 1:
+                weigh_and_store(jb - 1)
+        weigh_and_store(NB - 1)

@@ -111,12 +111,21 @@ def tile_neuromodulatedattentionwithelectrodes_kernel(tc, emb, q, k, v, offs, ou
         def normalise_and_flip(jb):
             nc.vector.reciprocal(e_sum[jb][:], e_sum[jb][:])
             p[jb] = held.tile([P, N], BF16, name=f"p{jb}")
-            nc.vector.tensor_scalar(p[jb][:], e[jb][:], e_sum[jb][:], None, MULT)
+            pieces = HALVES if jb == NB - 1 else 1
+            size = N // pieces
             for h in range(HALVES):
+                if h < pieces:
+                    columns = slice(h * size, (h + 1) * size)
+                    nc.vector.tensor_scalar(p[jb][:, columns], e[jb][:, columns], e_sum[jb][:], None, MULT)
                 pT_ps[jb, h] = flipped.tile([P, HB, P], BF16, name=f"pT_ps{jb}_{h}", tag="flip")
                 for hb in range(HB):
                     ib = h * HB + hb
                     nc.tensor.transpose(pT_ps[jb, h][:, hb, :], p[jb][:, ib * P : (ib + 1) * P], identity16[:])
+
+        def multiply(sums, cb, ib, pT):
+            nc.tensor.matmul(
+                sums, veT[cb][:, ib, :], pT[ib // HB][:, ib % HB, :], start=(ib == 0), stop=(ib == NB - 1)
+            )
 
         def weigh_and_store(jb):
             pT = {}
@@ -124,19 +133,24 @@ def tile_neuromodulatedattentionwithelectrodes_kernel(tc, emb, q, k, v, offs, ou
                 pT[h] = held.tile([P, HB, P], BF16, name=f"pT{jb}_{h}")
             nc.vector.tensor_copy(pT[0][:], pT_ps[jb, 0][:])
             nc.scalar.copy(pT[1][:], pT_ps[jb, 1][:])
-            o_ps = scores.tile([P, CB, P], F32, name=f"o_ps{jb}", tag="s_ps")
-            for cb in range(CB):
-                for ib in range(NB):
-                    nc.tensor.matmul(
-                        o_ps[:, cb, :],
-                        veT[cb][:, ib, :],
-                        pT[ib // HB][:, ib % HB, :],
-                        start=(ib == 0),
-                        stop=(ib == NB - 1),
-                    )
-            o = held.tile([P, CB, P], F32, name=f"o{jb}")
-            nc.scalar.copy(o[:], o_ps[:])
-            nc.sync.dma_start(out_blocks[:, :, jb * P : (jb + 1) * P], o[:])
+            if jb < NB - 1:
+                o_ps = scores.tile([P, CB, P], F32, name=f"o_ps{jb}", tag="s_ps")
+                for cb in range(CB):
+                    for ib in range(NB):
+                        multiply(o_ps[:, cb, :], cb, ib, pT)
+                o = held.tile([P, CB, P], F32, name=f"o{jb}")
+                nc.scalar.copy(o[:], o_ps[:])
+                nc.sync.dma_start(out_blocks[:, :, jb * P : (jb + 1) * P], o[:])
+            else:
+                last_ps = [scores.tile([P, P], F32, name=f"last_ps{cb}", tag="s_ps") for cb in range(CB)]
+                for h in range(HALVES):
+                    for cb in range(CB):
+                        for ib in range(h * HB, (h + 1) * HB):
+                            multiply(last_ps[cb][:], cb, ib, pT)
+                for cb, copy in enumerate((nc.vector.tensor_copy, nc.scalar.copy)):
+                    o_last = held.tile([P, P], F32, name=f"o_last{cb}")
+                    copy(o_last[:], last_ps[cb][:])
+                    nc.sync.dma_start(out_blocks[:, cb, jb * P : (jb + 1) * P], o_last[:])
 
         for jb in range(NB):
             measure(jb)

import math

import concourse.mybir as mybir
from concourse.masks import make_identity

P = 128
C, S, N = 256, 2048, 512
CB = C // P
NB = N // P
HALVES = 2
HB = NB // HALVES
EPS = 1e-6

FLOPS = 2 * 2 * N * N * C
BYTES = 4 * (C * N + 3 * C * N + C * N) + 2 * P * (N // 16)

F32, BF16, U16 = mybir.dt.float32, mybir.dt.bfloat16, mybir.dt.uint16
ADD, MULT, POW = mybir.AluOpType.add, mybir.AluOpType.mult, mybir.AluOpType.pow
EXP = mybir.ActivationFunctionType.Exp


def tile_neuromodulatedattentionwithelectrodes_kernel(tc, emb, q, k, v, offs, out):
    nc = tc.nc
    with (
        tc.tile_pool(name="held", bufs=1) as held,
        tc.psum_pool(name="scores", bufs=NB) as scores,
        tc.psum_pool(name="flipped", bufs=NB) as flipped,
    ):
        offsets = held.tile([P, N // 16], U16, name="offsets")
        nc.sync.dma_start(offsets[:], offs)
        table = [held.tile([P, S], F32, name=f"table{cb}") for cb in range(CB)]
        plain = {
            (name, cb): held.tile([P, N], F32, name=f"{name}{cb}") for name in "kqv" for cb in range(CB)
        }
        for cb in range(CB):
            channels = slice(cb * P, (cb + 1) * P)
            nc.sync.dma_start(table[cb][:], emb[channels, :])
            for name, source in (("k", k), ("q", q)):
                nc.sync.dma_start(plain[name, cb][:], source[channels, :])
        for cb in range(CB):
            nc.sync.dma_start(plain["v", cb][:], v[cb * P : (cb + 1) * P, :])

        identity32 = held.tile([P, P], F32, name="identity32")
        make_identity(nc, identity32[:])
        identity16 = held.tile([P, P], BF16, name="identity16")
        make_identity(nc, identity16[:])
        half = held.tile([P, 1], F32, name="half")
        nc.gpsimd.memset(half[:], 0.5)
        warm = held.tile([P, 1], F32, name="warm")
        nc.scalar.activation(warm[:], half[:], EXP)

        summed = {}
        rounded = {}
        veT = []
        s_ps = [scores.tile([P, N], F32, name=f"s_ps{jb}", tag="s_ps") for jb in range(NB)]
        for cb in range(CB):
            for name in "kq":
                summed[name, cb] = held.tile([P, N], F32, name=f"{name}e32_{cb}")
                nc.vector.tensor_tensor(
                    summed[name, cb][:], table[cb][:].indirect(offsets[:]), plain[name, cb][:], ADD
                )
            for name in "kq":
                rounded[name, cb] = held.tile([P, N], BF16, name=f"{name}e16_{cb}")
                nc.scalar.copy(rounded[name, cb][:], summed[name, cb][:])
            for jb in range(NB):
                nc.tensor.matmul(
                    s_ps[jb][:],
                    rounded["q", cb][:, jb * P : (jb + 1) * P],
                    rounded["k", cb][:],
                    start=(cb == 0),
                    stop=(cb == CB - 1),
                )
        for cb in range(CB):
            summed["v", cb] = held.tile([P, N], F32, name=f"ve32_{cb}")
            nc.vector.tensor_tensor(summed["v", cb][:], table[cb][:].indirect(offsets[:]), plain["v", cb][:], ADD)
            veT_ps = flipped.tile([P, NB, P], F32, name="veT_ps", tag="flip")
            for ib in range(NB):
                nc.tensor.transpose(veT_ps[:, ib, :], summed["v", cb][:, ib * P : (ib + 1) * P], identity32[:])
            veT.append(held.tile([P, NB, P], BF16, name=f"veT{cb}"))
            nc.scalar.copy(veT[cb][:], veT_ps[:])

        idle_ps = flipped.tile([P, N], F32, name="idle_ps", tag="flip")
        for repeat in range(12):
            nc.tensor.matmul(idle_ps[:], identity16[:], rounded["k", CB - 1][:], start=True, stop=True)

        mean_var, root, gain, shift, e, e_sum, p, pT_ps = {}, {}, {}, {}, {}, {}, {}, {}
        out_blocks = out.rearrange("(cb p) j -> p cb j", p=P)

        def measure(jb):
            stats = held.tile([P, 6], F32, name=f"stats{jb}")
            nc.vector.bn_stats(stats[:], s_ps[jb][:])
            mean_var[jb] = held.tile([P, 2], F32, name=f"mean_var{jb}")
            nc.vector.bn_aggr(mean_var[jb][:], stats[:])
            root[jb] = held.tile([P, 1], F32, name=f"root{jb}")
            nc.gpsimd.tensor_tensor(root[jb][:], mean_var[jb][:, 1:2], half[:], POW)

        def exponentiate(jb):
            gain[jb] = held.tile([P, 1], F32, name=f"gain{jb}")
            nc.vector.tensor_scalar(
                gain[jb][:], root[jb][:], math.sqrt(N / (N - 1)), math.sqrt(C) * EPS, MULT, ADD
            )
            nc.vector.reciprocal(gain[jb][:], gain[jb][:])
            shift[jb] = held.tile([P, 1], F32, name=f"shift{jb}")
            nc.vector.tensor_scalar(shift[jb][:], mean_var[jb][:, 0:1], gain[jb][:], -1.0, MULT, MULT)
            e[jb] = held.tile([P, N], F32, name=f"e{jb}")
            e_sum[jb] = held.tile([P, 1], F32, name=f"e_sum{jb}")
            nc.scalar.activation(
                e[jb][:], s_ps[jb][:], EXP, bias=shift[jb][:], scale=gain[jb][:], accum_out=e_sum[jb][:]
            )

        def normalise_and_flip(jb):
            nc.vector.reciprocal(e_sum[jb][:], e_sum[jb][:])
            p[jb] = held.tile([P, N], BF16, name=f"p{jb}")
            pieces = HALVES if jb == NB - 1 else 1
            size = N // pieces
            for h in range(HALVES):
                if h < pieces:
                    columns = slice(h * size, (h + 1) * size)
                    nc.vector.tensor_scalar(p[jb][:, columns], e[jb][:, columns], e_sum[jb][:], None, MULT)
                pT_ps[jb, h] = flipped.tile([P, HB, P], BF16, name=f"pT_ps{jb}_{h}", tag="flip")
                for hb in range(HB):
                    ib = h * HB + hb
                    nc.tensor.transpose(pT_ps[jb, h][:, hb, :], p[jb][:, ib * P : (ib + 1) * P], identity16[:])

        def multiply(sums, cb, ib, pT):
            nc.tensor.matmul(
                sums, veT[cb][:, ib, :], pT[ib // HB][:, ib % HB, :], start=(ib == 0), stop=(ib == NB - 1)
            )

        def weigh_and_store(jb):
            pT = {}
            for h in range(HALVES):
                pT[h] = held.tile([P, HB, P], BF16, name=f"pT{jb}_{h}")
            nc.vector.tensor_copy(pT[0][:], pT_ps[jb, 0][:])
            nc.scalar.copy(pT[1][:], pT_ps[jb, 1][:])
            if jb < NB - 1:
                o_ps = scores.tile([P, CB, P], F32, name=f"o_ps{jb}", tag="s_ps")
                for cb in range(CB):
                    for ib in range(NB):
                        multiply(o_ps[:, cb, :], cb, ib, pT)
                o = held.tile([P, CB, P], F32, name=f"o{jb}")
                nc.scalar.copy(o[:], o_ps[:])
                nc.sync.dma_start(out_blocks[:, :, jb * P : (jb + 1) * P], o[:])
            else:
                last_ps = [scores.tile([P, P], F32, name=f"last_ps{cb}", tag="s_ps") for cb in range(CB)]
                for h in range(HALVES):
                    for cb in range(CB):
                        for ib in range(h * HB, (h + 1) * HB):
                            multiply(last_ps[cb][:], cb, ib, pT)
                for cb, copy in enumerate((nc.vector.tensor_copy, nc.scalar.copy)):
                    o_last = held.tile([P, P], F32, name=f"o_last{cb}")
                    copy(o_last[:], last_ps[cb][:])
                    nc.sync.dma_start(out_blocks[:, cb, jb * P : (jb + 1) * P], o_last[:])

        for jb in range(NB):
            measure(jb)
        for jb in range(NB):
            exponentiate(jb)
        for jb in range(NB):
            normalise_and_flip(jb)
            if jb >= 1:
                weigh_and_store(jb - 1)
        weigh_and_store(NB - 1)
